import numpy as np
import ml_dtypes


def mxq(x, axis, fmt="e4m3"):
    dtype, down = {"e4m3": (ml_dtypes.float8_e4m3fn, 7), "e5m2": (ml_dtypes.float8_e5m2, 14)}[fmt]
    v = np.moveaxis(np.asarray(x, np.float32).astype(ml_dtypes.bfloat16).astype(np.float64), axis, -1)
    blocks = v.reshape(v.shape[:-1] + (-1, 32))
    amax = np.abs(blocks).max(-1, keepdims=True)
    byte = np.maximum(np.where(amax > 0, np.frexp(amax)[1] - 1 + 127, 0) - down, 1)
    scale = np.exp2(byte - 127.0)
    codes = (blocks / scale).astype(np.float32).astype(dtype).astype(np.float64)
    return np.moveaxis((codes * scale).reshape(v.shape), -1, axis)


WIDE = False


def mx_kscale(k):
    if not WIDE:
        return np.ones(k)
    levels = np.array([10, -10, 5, -5, 0])
    if k % 512:
        return np.exp2(np.random.permutation(np.resize(levels, k // 32))).repeat(32)
    a = np.empty((k // 512, 16))
    for p in range(k // 512):
        a[p, :8] = np.random.permutation(np.resize(levels, 8))
        for g in range(8):
            far = levels[np.abs(levels - a[p, g]) >= 10]
            a[p, g + 8] = far[np.random.randint(len(far))]
    return np.exp2(a.ravel()).repeat(32)


BF16 = ml_dtypes.bfloat16


def bf(x):
    return np.asarray(x, np.float32).astype(BF16)


def f64(x):
    return np.asarray(x).astype(np.float64)


P, N, Z, H1, H2, C = 8, 256, 16, 512, 2048, 256
EPS = 1e-5


def batch_norm(h, gamma, beta):
    mu = h.mean(axis=1, keepdims=True)
    var = h.var(axis=1, keepdims=True)
    return (h - mu) * (1.0 / np.sqrt(var + EPS)) * gamma[:, None, :] + beta[:, None, :]


def setup_inputs():
    r = np.random.standard_normal
    t = mx_kscale(H1)
    sd = np.where(np.random.random((P, 1, H1)) < 0.25, np.sqrt(EPS), 1.0)
    return {"h6_pre": bf((r((P, N, H1)) + 0.5 * r((P, 1, H1))) * sd),
            "g6": bf((1.0 + 0.1 * r((P, H1))) * t),
            "be6": bf(0.3 * r((P, H1)) * t),
            "W7": bf(r((P, H2, H1)) / np.sqrt(H1) / t),
            "b7": bf(0.3 * r((P, H2)))}


def reference(h6_pre, g6, be6, W7, b7):
    a = np.maximum(batch_norm(f64(h6_pre), f64(g6), f64(be6)), 0.0)
    y = mxq(a, 2, "e4m3") @ mxq(f64(W7), 2, "e4m3").transpose(0, 2, 1)
    return y + f64(b7)[:, None, :]

@@ -1,0 +1,303 @@
+from contextlib import ExitStack
+
+import concourse.mybir as mybir
+from concourse.masks import make_identity
+
+F32 = mybir.dt.float32
+BF16 = mybir.dt.bfloat16
+U32 = mybir.dt.uint32
+U8 = mybir.dt.uint8
+FP8X4 = mybir.dt.float8_e4m3fn_x4
+ACT = mybir.ActivationFunctionType
+ALU = mybir.AluOpType
+
+P = 128
+BLOCKS, ROWS, K, COLS = 8, 256, 512, 2048
+EPS = 1e-5
+FLOPS = 2 * BLOCKS * ROWS * K * COLS
+
+PACK = 4
+WORDS = K // 2
+BANK = 512
+STEP = 512
+HALF = 2 * STEP
+STEPS = BLOCKS * COLS // STEP
+HALVES = BLOCKS * COLS // HALF
+W_AHEAD = 8
+LAG = 2
+G_ROW, BE_ROW = STEPS, STEPS + BLOCKS
+SMALL = STEPS + 2 * BLOCKS
+FINE_STORES = HALVES - 2
+
+
+def tile_decoder_pa_kernel(tc, h6_pre, g6, be6, W7, b7, out):
+    nc = tc.nc
+    with ExitStack() as ctx:
+        keep = ctx.enter_context(tc.tile_pool(name="keep", bufs=1))
+        w_pool = ctx.enter_context(tc.tile_pool(name="w_rows", bufs=W_AHEAD))
+        grouped_pool = ctx.enter_context(tc.tile_pool(name="w_grouped", bufs=6))
+        code_pool = ctx.enter_context(tc.tile_pool(name="w_codes", bufs=6))
+        a_pool = ctx.enter_context(tc.tile_pool(name="a_values", bufs=2))
+        bias_pool = ctx.enter_context(tc.tile_pool(name="bias", bufs=3))
+        out_pool = ctx.enter_context(tc.tile_pool(name="out_tiles", bufs=4))
+        flip_pool = ctx.enter_context(tc.psum_pool(name="flipped", bufs=4))
+        acc_pool = ctx.enter_context(tc.psum_pool(name="sums", bufs=4))
+        ctx.enter_context(tc.manual_schedule())
+
+        ident = keep.tile([P, P], F32, name="ident")
+        make_identity(nc, ident[:])
+        minus_half = keep.tile([P, PACK], F32, name="minus_half")
+        nc.gpsimd.memset(minus_half[:], -0.5)
+
+        h_rows = keep.tile([P, BLOCKS * 2 * K], BF16, name="h_rows")
+        h_words = h_rows[:].bitcast(F32)
+
+        def load_h(first, last):
+            nc.sync.dma_start(
+                out=h_rows[:, first * 2 * K : last * 2 * K].rearrange("p (b l k) -> p b l k", l=2, k=K),
+                in_=h6_pre[first:last].rearrange("b (m l) k -> m b l k", l=2),
+            )
+
+        w_rows = {}
+
+        def load_w(half):
+            b, side = divmod(half, 2)
+            tile = w_pool.tile([P, HALF * K // P], BF16, name="w_rows")
+            nc.sync.dma_start(
+                out=tile[:].rearrange("p (q a k) -> p q a k", q=2, a=4),
+                in_=W7[b].rearrange("(q c a) k -> c q a k", q=4, c=P)[:, 2 * side : 2 * side + 2],
+            )
+            w_rows[half] = tile
+
+        small_rows = keep.tile([P, K], BF16, name="small_rows")
+        nc.vector.memset(small_rows[32:64, :], 0.0)
+        nc.vector.memset(small_rows[64:128, :], 0.0)
+        load_h(0, 1)
+        nc.sync.dma_start(out=small_rows[G_ROW : G_ROW + BLOCKS, :], in_=g6)
+        nc.sync.dma_start(out=small_rows[BE_ROW : BE_ROW + BLOCKS, :], in_=be6)
+        nc.sync.dma_start(out=small_rows[0:STEPS, :], in_=b7.rearrange("b (q w) -> (b q) w", w=STEP))
+        load_h(1, 2)
+        load_h(2, 4)
+        load_w(0)
+        load_h(4, 6)
+        load_w(1)
+        load_h(6, 8)
+        for half in range(2, W_AHEAD):
+            load_w(half)
+
+        stats = keep.tile([P, BLOCKS * PACK * 3], F32, name="stats")
+        stats_view = stats[:].rearrange("p (i c) -> p i c", c=3)
+        var_eps = keep.tile([P, BLOCKS * PACK], F32, name="var_eps")
+        inv_std = keep.tile([P, BLOCKS * PACK], F32, name="inv_std")
+        scale = keep.tile([P, BLOCKS * PACK], F32, name="scale")
+        mean_scaled = keep.tile([P, BLOCKS * PACK], F32, name="mean_scaled")
+        shift = keep.tile([P, BLOCKS * PACK], F32, name="shift")
+        small_cols = keep.tile([P, 2 * SMALL], F32, name="small_cols")
+        small_values = small_cols[:].bitcast(BF16)
+        h_flipped = {}
+        a_planes = {}
+        a_grouped = {}
+        a_codes = {}
+
+        def transpose_h(b):
+            bank = flip_pool.tile([P, BANK], F32, name="bank", tag="bank")
+            for u in range(2):
+                for l in range(2):
+                    first = (b * 2 + l) * WORDS
+                    nc.tensor.transpose(
+                        out=bank[:, (u * 2 + l) * P : (u * 2 + l + 1) * P],
+                        in_=h_words[:, first + u : first + WORDS : 2],
+                        identity=ident[:],
+                    )
+            flipped = keep.tile([P, BANK], F32, name="h_flipped%d" % b)
+            nc.scalar.copy(out=flipped[:], in_=bank[:])
+            h_flipped[b] = flipped[:].bitcast(BF16)
+
+        def transpose_small():
+            bank = flip_pool.tile([P, BANK], F32, name="bank", tag="bank")
+            for u in range(2):
+                nc.tensor.transpose(
+                    out=bank[:, u * P : (u + 1) * P], in_=small_rows[:].bitcast(F32)[:, u:WORDS:2], identity=ident[:]
+                )
+            nc.scalar.copy(
+                out=small_cols[:].rearrange("p (r u) -> p r u", u=2),
+                in_=bank[:, 0 : 2 * P].rearrange("p (u r) -> p r u", u=2)[:, 0:SMALL, :],
+            )
+
+        def statistics(b):
+            for u in range(2):
+                nc.vector.bn_stats(
+                    out=stats[:, (b * 2 + u) * 6 : (b * 2 + u + 1) * 6],
+                    in_=h_flipped[b][:, u * 2 * ROWS : (u + 1) * 2 * ROWS],
+                )
+            four = slice(PACK * b, PACK * b + PACK)
+            g_four = slice(PACK * (G_ROW + b), PACK * (G_ROW + b + 1))
+            be_four = slice(PACK * (BE_ROW + b), PACK * (BE_ROW + b + 1))
+            nc.gpsimd.tensor_scalar(
+                out=var_eps[:, four], in0=stats_view[:, four, 2], scalar1=1.0 / ROWS, scalar2=EPS,
+                op0=ALU.mult, op1=ALU.add,
+            )
+            nc.gpsimd.tensor_tensor(out=inv_std[:, four], in0=var_eps[:, four], in1=minus_half[:], op=ALU.pow)
+            nc.gpsimd.tensor_tensor(out=scale[:, four], in0=inv_std[:, four], in1=small_values[:, g_four], op=ALU.mult)
+            nc.gpsimd.tensor_tensor(
+                out=mean_scaled[:, four], in0=stats_view[:, four, 1], in1=scale[:, four], op=ALU.mult
+            )
+            nc.gpsimd.tensor_tensor(
+                out=shift[:, four],
+                in0=small_values[:, be_four],
+                in1=mean_scaled[:, four],
+                op=ALU.subtract,
+            )
+
+        def normalise(b):
+            planes = a_pool.tile([P, PACK * ROWS], BF16, name="a_planes")
+            for u in range(2):
+                pairs = h_flipped[b][:, u * 2 * ROWS : (u + 1) * 2 * ROWS].rearrange("p (n e) -> p n e", e=2)
+                for e in range(2):
+                    t = 2 * u + e
+                    nc.scalar.activation(
+                        out=planes[:, t * ROWS : (t + 1) * ROWS],
+                        in_=pairs[:, :, e],
+                        func=ACT.Relu,
+                        scale=scale[:, PACK * b + t : PACK * b + t + 1],
+                        bias=shift[:, PACK * b + t : PACK * b + t + 1],
+                    )
+            a_planes[b] = planes
+
+        def regroup(b):
+            grouped = a_pool.tile([P, ROWS * PACK], BF16, name="a_grouped", align_bytes=64)
+            copy = nc.scalar.copy if b % 2 == 1 else nc.vector.tensor_copy
+            copy(
+                out=grouped[:].rearrange("p (c i t) -> p c t i", i=4, t=PACK),
+                in_=a_planes[b][:].rearrange("p (t c i) -> p c t i", t=PACK, i=4),
+            )
+            a_grouped[b] = grouped
+
+        def quantise_a(b):
+            codes = keep.tile([P, ROWS], U32, name="a_codes%d" % b, align_bytes=64)
+            scales = keep.tile([P, ROWS], U8, name="a_scales%d" % b, align_bytes=64)
+            nc.vector.quantize_mx(out=codes[:].bitcast(FP8X4), scales=scales[:], in_=a_grouped[b][:])
+            a_codes[b] = (codes, scales)
+
+        bias_tiles = {}
+        w_grouped = {}
+        w_codes = {}
+        out_tiles = {}
+
+        def spread_bias(half):
+            bank = flip_pool.tile([P, BANK], F32, name="bank", tag="bank")
+            for i in range(4):
+                column = 4 * half + i
+                nc.tensor.transpose(
+                    out=bank[:, i * P : (i + 1) * P],
+                    in_=small_cols[:, column : column + 1].to_broadcast([P, P]),
+                    identity=ident[:],
+                )
+            spread = bias_pool.tile([P, BANK], F32, name="bias")
+            nc.scalar.copy(
+                out=spread[:].rearrange("p (q c u) -> p q c u", q=2, u=2),
+                in_=bank[:].rearrange("p (q u c) -> p q c u", q=2, u=2),
+            )
+            bias_tiles[half] = spread[:].bitcast(BF16)
+
+        def transpose_w(step, copy):
+            half, q = divmod(step, 2)
+            if q == 0:
+                spread_bias(half)
+            words = w_rows[half][:].bitcast(F32)
+            grouped = grouped_pool.tile([P, STEP * PACK], BF16, name="w_grouped", align_bytes=64)
+            grouped_words = grouped[:].bitcast(F32)
+            for pair in range(2):
+                bank = flip_pool.tile([P, BANK], F32, name="bank", tag="bank")
+                for a in range(2):
+                    for u in range(2):
+                        first = (q * 4 + 2 * pair + a) * WORDS
+                        nc.tensor.transpose(
+                            out=bank[:, (a * 2 + u) * P : (a * 2 + u + 1) * P],
+                            in_=words[:, first + u : first + WORDS : 2],
+                            identity=ident[:],
+                        )
+                copy(
+                    out=grouped_words[:, pair * BANK : (pair + 1) * BANK].rearrange("p (a c u) -> p a c u", a=2, u=2),
+                    in_=bank[:].rearrange("p (a u c) -> p a c u", a=2, u=2),
+                )
+            w_grouped[step] = grouped
+
+        def quantise_w(step):
+            codes = code_pool.tile([P, STEP], U32, name="w_codes", align_bytes=64)
+            scales = code_pool.tile([P, STEP], U8, name="w_scales", align_bytes=64)
+            nc.vector.quantize_mx(out=codes[:].bitcast(FP8X4), scales=scales[:], in_=w_grouped[step][:])
+            w_codes[step] = (codes, scales)
+
+        def multiply(step):
+            half, q = divmod(step, 2)
+            b, side = divmod(half, 2)
+            codes, scales = a_codes[b]
+            moving, moving_scales = w_codes[step]
+            if q == 0:
+                out_tiles[half] = out_pool.tile([P, 2 * HALF], F32, name="out_tile")
+            tile = out_tiles[half]
+            rows = out[b].rearrange("(m l) j -> m l j", l=2)
+            first_col = side * HALF + q * STEP
+            for l in range(2):
+                acc = acc_pool.tile([P, BANK], F32, name="acc")
+                nc.tensor.matmul_mx(
+                    out=acc[:],
+                    lhsT=codes[:, l * P : (l + 1) * P].bitcast(FP8X4),
+                    lhsT_scale=scales[:, l * P : (l + 1) * P],
+                    rhs=moving[:].bitcast(FP8X4),
+                    rhs_scale=moving_scales[:],
+                    start=True,
+                    stop=True,
+                )
+                part = tile[:, l * HALF + q * STEP : l * HALF + (q + 1) * STEP]
+                nc.vector.tensor_tensor(
+                    out=part.rearrange("p (c a) -> p c a", a=4),
+                    in0=acc[:].rearrange("p (a c) -> p c a", a=4),
+                    in1=bias_tiles[half][:, q * STEP : (q + 1) * STEP].rearrange("p (c a) -> p c a", a=4),
+                    op=ALU.add,
+                )
+                if step == STEPS - 1:
+                    nc.sync.dma_start(out=rows[:, l, first_col : first_col + STEP], in_=part)
+            both = tile[:].rearrange("p (l j) -> p l j", l=2)
+            if half >= FINE_STORES and step < STEPS - 1:
+                nc.sync.dma_start(
+                    out=rows[:, :, first_col : first_col + STEP], in_=both[:, :, q * STEP : (q + 1) * STEP]
+                )
+            if half < FINE_STORES and q == 1:
+                nc.sync.dma_start(out=rows[:, :, side * HALF : (side + 1) * HALF], in_=both)
+
+        transpose_h(0)
+        transpose_small()
+        statistics(0)
+        for b in range(1, 4):
+            transpose_h(b)
+            statistics(b)
+        transpose_w(0, nc.scalar.copy)
+        quantise_w(0)
+        normalise(0)
+        transpose_w(1, nc.vector.tensor_copy)
+        load_w(W_AHEAD)
+        regroup(0)
+        quantise_a(0)
+        quantise_w(1)
+        prepare_from = [max(2, 4 * b - 3) for b in range(BLOCKS)]
+        for step in range(2, STEPS):
+            transpose_w(step, nc.scalar.copy)
+            quantise_w(step)
+            if step < 6:
+                transpose_h(step + 2)
+            multiply(step - LAG)
+            if step % 2 == 1 and step // 2 + W_AHEAD < HALVES:
+                load_w(step // 2 + W_AHEAD)
+            for b in range(1, BLOCKS):
+                if step == prepare_from[b]:
+                    normalise(b)
+                if step == prepare_from[b] + 1:
+                    regroup(b)
+                if step == prepare_from[b] + 2:
+                    quantise_a(b)
+            if step < 6:
+                statistics(step + 2)
+        for step in range(STEPS - LAG, STEPS):
+            multiply(step)

@@ -40,6 +40,7 @@ def tile_decoder_pa_kernel(tc, h6_pre, g6, be6, W7, b7, out):
         a_pool = ctx.enter_context(tc.tile_pool(name="a_values", bufs=2))
         bias_pool = ctx.enter_context(tc.tile_pool(name="bias", bufs=3))
         out_pool = ctx.enter_context(tc.tile_pool(name="out_tiles", bufs=4))
+        fine_pool = ctx.enter_context(tc.tile_pool(name="fine_out_tiles", bufs=4))
         flip_pool = ctx.enter_context(tc.psum_pool(name="flipped", bufs=4))
         acc_pool = ctx.enter_context(tc.psum_pool(name="sums", bufs=4))
         ctx.enter_context(tc.manual_schedule())
@@ -234,9 +235,13 @@ def tile_decoder_pa_kernel(tc, h6_pre, g6, be6, W7, b7, out):
             b, side = divmod(half, 2)
             codes, scales = a_codes[b]
             moving, moving_scales = w_codes[step]
-            if q == 0:
-                out_tiles[half] = out_pool.tile([P, 2 * HALF], F32, name="out_tile")
-            tile = out_tiles[half]
+            fine = half >= FINE_STORES
+            if fine:
+                tile = fine_pool.tile([P, 2 * STEP], F32, name="fine_tile")
+            else:
+                if q == 0:
+                    out_tiles[half] = out_pool.tile([P, 2 * HALF], F32, name="out_tile")
+                tile = out_tiles[half]
             rows = out[b].rearrange("(m l) j -> m l j", l=2)
             first_col = side * HALF + q * STEP
             for l in range(2):
@@ -250,7 +255,8 @@ def tile_decoder_pa_kernel(tc, h6_pre, g6, be6, W7, b7, out):
                     start=True,
                     stop=True,
                 )
-                part = tile[:, l * HALF + q * STEP : l * HALF + (q + 1) * STEP]
+                first = l * STEP if fine else l * HALF + q * STEP
+                part = tile[:, first : first + STEP]
                 nc.vector.tensor_tensor(
                     out=part.rearrange("p (c a) -> p c a", a=4),
                     in0=acc[:].rearrange("p (a c) -> p c a", a=4),
@@ -260,11 +266,9 @@ def tile_decoder_pa_kernel(tc, h6_pre, g6, be6, W7, b7, out):
                 if step == STEPS - 1:
                     nc.sync.dma_start(out=rows[:, l, first_col : first_col + STEP], in_=part)
             both = tile[:].rearrange("p (l j) -> p l j", l=2)
-            if half >= FINE_STORES and step < STEPS - 1:
-                nc.sync.dma_start(
-                    out=rows[:, :, first_col : first_col + STEP], in_=both[:, :, q * STEP : (q + 1) * STEP]
-                )
-            if half < FINE_STORES and q == 1:
+            if fine and step < STEPS - 1:
+                nc.sync.dma_start(out=rows[:, :, first_col : first_col + STEP], in_=both)
+            if not fine and q == 1:
                 nc.sync.dma_start(out=rows[:, :, side * HALF : (side + 1) * HALF], in_=both)
 
         transpose_h(0)

@@ -27,7 +27,6 @@ W_AHEAD = 8
 LAG = 2
 G_ROW, BE_ROW = STEPS, STEPS + BLOCKS
 SMALL = STEPS + 2 * BLOCKS
-FINE_STORES = HALVES - 2
 
 
 def tile_decoder_pa_kernel(tc, h6_pre, g6, be6, W7, b7, out):
@@ -39,8 +38,7 @@ def tile_decoder_pa_kernel(tc, h6_pre, g6, be6, W7, b7, out):
         code_pool = ctx.enter_context(tc.tile_pool(name="w_codes", bufs=6))
         a_pool = ctx.enter_context(tc.tile_pool(name="a_values", bufs=2))
         bias_pool = ctx.enter_context(tc.tile_pool(name="bias", bufs=3))
-        out_pool = ctx.enter_context(tc.tile_pool(name="out_tiles", bufs=4))
-        fine_pool = ctx.enter_context(tc.tile_pool(name="fine_out_tiles", bufs=4))
+        out_pool = ctx.enter_context(tc.tile_pool(name="out_tiles", bufs=3))
         flip_pool = ctx.enter_context(tc.psum_pool(name="flipped", bufs=4))
         acc_pool = ctx.enter_context(tc.psum_pool(name="sums", bufs=4))
         ctx.enter_context(tc.manual_schedule())
@@ -65,8 +63,8 @@ def tile_decoder_pa_kernel(tc, h6_pre, g6, be6, W7, b7, out):
             b, side = divmod(half, 2)
             tile = w_pool.tile([P, HALF * K // P], BF16, name="w_rows")
             nc.sync.dma_start(
-                out=tile[:].rearrange("p (q a k) -> p q a k", q=2, a=4),
-                in_=W7[b].rearrange("(q c a) k -> c q a k", q=4, c=P)[:, 2 * side : 2 * side + 2],
+                out=tile[:].rearrange("p (i k) -> p i k", k=K),
+                in_=W7[b].rearrange("(d c i) k -> d c i k", d=2, c=P)[side],
             )
             w_rows[half] = tile
 
@@ -235,15 +233,16 @@ def tile_decoder_pa_kernel(tc, h6_pre, g6, be6, W7, b7, out):
             b, side = divmod(half, 2)
             codes, scales = a_codes[b]
             moving, moving_scales = w_codes[step]
-            fine = half >= FINE_STORES
+            fine = b == BLOCKS - 1
             if fine:
-                tile = fine_pool.tile([P, 2 * STEP], F32, name="fine_tile")
-            else:
                 if q == 0:
                     out_tiles[half] = out_pool.tile([P, 2 * HALF], F32, name="out_tile")
                 tile = out_tiles[half]
+            else:
+                if side == 0 and q == 0:
+                    out_tiles[b] = out_pool.tile([P, 2 * COLS], F32, name="out_tile")
+                tile = out_tiles[b]
             rows = out[b].rearrange("(m l) j -> m l j", l=2)
-            first_col = side * HALF + q * STEP
             for l in range(2):
                 acc = acc_pool.tile([P, BANK], F32, name="acc")
                 nc.tensor.matmul_mx(
@@ -255,21 +254,18 @@ def tile_decoder_pa_kernel(tc, h6_pre, g6, be6, W7, b7, out):
                     start=True,
                     stop=True,
                 )
-                first = l * STEP if fine else l * HALF + q * STEP
-                part = tile[:, first : first + STEP]
+                first = l * HALF if fine else l * COLS + side * HALF
+                part = tile[:, first : first + HALF]
                 nc.vector.tensor_tensor(
-                    out=part.rearrange("p (c a) -> p c a", a=4),
+                    out=part.rearrange("p (c q a) -> p q c a", q=2, a=4)[:, q],
                     in0=acc[:].rearrange("p (a c) -> p c a", a=4),
-                    in1=bias_tiles[half][:, q * STEP : (q + 1) * STEP].rearrange("p (c a) -> p c a", a=4),
+                    in1=bias_tiles[half].rearrange("p (c q a) -> p q c a", q=2, a=4)[:, q],
                     op=ALU.add,
                 )
-                if step == STEPS - 1:
-                    nc.sync.dma_start(out=rows[:, l, first_col : first_col + STEP], in_=part)
-            both = tile[:].rearrange("p (l j) -> p l j", l=2)
-            if fine and step < STEPS - 1:
-                nc.sync.dma_start(out=rows[:, :, first_col : first_col + STEP], in_=both)
-            if not fine and q == 1:
-                nc.sync.dma_start(out=rows[:, :, side * HALF : (side + 1) * HALF], in_=both)
+                if fine and q == 1:
+                    nc.sync.dma_start(out=rows[:, l, side * HALF : (side + 1) * HALF], in_=part)
+            if not fine and side == 1 and q == 1:
+                nc.sync.dma_start(out=rows, in_=tile[:].rearrange("p (l j) -> p l j", l=2))
 
         transpose_h(0)
         transpose_small()

@@ -24,6 +24,7 @@ HALF = 2 * STEP
 STEPS = BLOCKS * COLS // STEP
 HALVES = BLOCKS * COLS // HALF
 W_AHEAD = 8
+STORE_WIDTHS = [COLS] * (BLOCKS - 2) + [HALF, STEP]
 LAG = 2
 G_ROW, BE_ROW = STEPS, STEPS + BLOCKS
 SMALL = STEPS + 2 * BLOCKS
@@ -62,10 +63,16 @@ def tile_decoder_pa_kernel(tc, h6_pre, g6, be6, W7, b7, out):
         def load_w(half):
             b, side = divmod(half, 2)
             tile = w_pool.tile([P, HALF * K // P], BF16, name="w_rows")
-            nc.sync.dma_start(
-                out=tile[:].rearrange("p (i k) -> p i k", k=K),
-                in_=W7[b].rearrange("(d c i) k -> d c i k", d=2, c=P)[side],
-            )
+            if b < BLOCKS - 1:
+                nc.sync.dma_start(
+                    out=tile[:].rearrange("p (i k) -> p i k", k=K),
+                    in_=W7[b].rearrange("(d c i) k -> d c i k", d=2, c=P)[side],
+                )
+            else:
+                nc.sync.dma_start(
+                    out=tile[:].rearrange("p (q a k) -> p q a k", q=2, a=4),
+                    in_=W7[b].rearrange("(q c a) k -> c q a k", q=4, c=P)[:, 2 * side : 2 * side + 2],
+                )
             w_rows[half] = tile
 
         small_rows = keep.tile([P, K], BF16, name="small_rows")
@@ -233,15 +240,12 @@ def tile_decoder_pa_kernel(tc, h6_pre, g6, be6, W7, b7, out):
             b, side = divmod(half, 2)
             codes, scales = a_codes[b]
             moving, moving_scales = w_codes[step]
-            fine = b == BLOCKS - 1
-            if fine:
-                if q == 0:
-                    out_tiles[half] = out_pool.tile([P, 2 * HALF], F32, name="out_tile")
-                tile = out_tiles[half]
-            else:
-                if side == 0 and q == 0:
-                    out_tiles[b] = out_pool.tile([P, 2 * COLS], F32, name="out_tile")
-                tile = out_tiles[b]
+            width = STORE_WIDTHS[b]
+            col = side * HALF + q * STEP
+            if col % width == 0:
+                out_tiles[b] = out_pool.tile([P, 2 * width], F32, name="out_tile")
+            tile = out_tiles[b]
+            both = tile[:].rearrange("p (l j) -> p l j", l=2)
             rows = out[b].rearrange("(m l) j -> m l j", l=2)
             for l in range(2):
                 acc = acc_pool.tile([P, BANK], F32, name="acc")
@@ -254,18 +258,20 @@ def tile_decoder_pa_kernel(tc, h6_pre, g6, be6, W7, b7, out):
                     start=True,
                     stop=True,
                 )
-                first = l * HALF if fine else l * COLS + side * HALF
-                part = tile[:, first : first + HALF]
-                nc.vector.tensor_tensor(
-                    out=part.rearrange("p (c q a) -> p q c a", q=2, a=4)[:, q],
-                    in0=acc[:].rearrange("p (a c) -> p c a", a=4),
-                    in1=bias_tiles[half].rearrange("p (c q a) -> p q c a", q=2, a=4)[:, q],
-                    op=ALU.add,
-                )
-                if fine and q == 1:
-                    nc.sync.dma_start(out=rows[:, l, side * HALF : (side + 1) * HALF], in_=part)
-            if not fine and side == 1 and q == 1:
-                nc.sync.dma_start(out=rows, in_=tile[:].rearrange("p (l j) -> p l j", l=2))
+                sums = acc[:].rearrange("p (a c) -> p c a", a=4)
+                if width == STEP:
+                    part = both[:, l].rearrange("p (c a) -> p c a", a=4)
+                    bias = bias_tiles[half][:, q * STEP : (q + 1) * STEP].rearrange("p (c a) -> p c a", a=4)
+                else:
+                    first = side * HALF % width
+                    part = both[:, l, first : first + HALF].rearrange("p (c q a) -> p q c a", q=2, a=4)[:, q]
+                    bias = bias_tiles[half].rearrange("p (c q a) -> p q c a", q=2, a=4)[:, q]
+                nc.vector.tensor_tensor(out=part, in0=sums, in1=bias, op=ALU.add)
+                if step == STEPS - 1:
+                    nc.sync.dma_start(out=rows[:, l, col : col + STEP], in_=both[:, l])
+            end = col + STEP
+            if end % width == 0 and step < STEPS - 1:
+                nc.sync.dma_start(out=rows[:, :, end - width : end], in_=both)
 
         transpose_h(0)
         transpose_small()

@@ -24,6 +24,7 @@ HALF = 2 * STEP
 STEPS = BLOCKS * COLS // STEP
 HALVES = BLOCKS * COLS // HALF
 W_AHEAD = 8
+SPREAD_HALVES = 4
 STORE_WIDTHS = [COLS] * (BLOCKS - 2) + [HALF, STEP]
 LAG = 2
 G_ROW, BE_ROW = STEPS, STEPS + BLOCKS
@@ -40,12 +41,15 @@ def tile_decoder_pa_kernel(tc, h6_pre, g6, be6, W7, b7, out):
         a_pool = ctx.enter_context(tc.tile_pool(name="a_values", bufs=2))
         bias_pool = ctx.enter_context(tc.tile_pool(name="bias", bufs=3))
         out_pool = ctx.enter_context(tc.tile_pool(name="out_tiles", bufs=3))
+        fine_pool = ctx.enter_context(tc.tile_pool(name="fine_out_tiles", bufs=4))
         flip_pool = ctx.enter_context(tc.psum_pool(name="flipped", bufs=4))
         acc_pool = ctx.enter_context(tc.psum_pool(name="sums", bufs=4))
         ctx.enter_context(tc.manual_schedule())
 
         ident = keep.tile([P, P], F32, name="ident")
         make_identity(nc, ident[:])
+        ident_bf16 = keep.tile([P, P], BF16, name="ident_bf16")
+        nc.gpsimd.tensor_copy(out=ident_bf16[:], in_=ident[:])
         minus_half = keep.tile([P, PACK], F32, name="minus_half")
         nc.gpsimd.memset(minus_half[:], -0.5)
 
@@ -206,10 +210,25 @@ def tile_decoder_pa_kernel(tc, h6_pre, g6, be6, W7, b7, out):
             )
             bias_tiles[half] = spread[:].bitcast(BF16)
 
+        def select_bias(half):
+            bank = flip_pool.tile([P, HALF], BF16, name="bank", tag="bank")
+            for q in range(2):
+                row = 2 * half + q
+                nc.tensor.matmul(
+                    out=bank[:, q * STEP : (q + 1) * STEP],
+                    lhsT=ident_bf16[:, row : row + 1].to_broadcast([P, P]),
+                    rhs=small_rows[:],
+                    start=True,
+                    stop=True,
+                )
+            spread = bias_pool.tile([P, BANK], F32, name="bias")
+            nc.scalar.copy(out=spread[:], in_=bank[:].bitcast(F32))
+            bias_tiles[half] = spread[:].bitcast(BF16)
+
         def transpose_w(step, copy):
             half, q = divmod(step, 2)
             if q == 0:
-                spread_bias(half)
+                (spread_bias if half < SPREAD_HALVES else select_bias)(half)
             words = w_rows[half][:].bitcast(F32)
             grouped = grouped_pool.tile([P, STEP * PACK], BF16, name="w_grouped", align_bytes=64)
             grouped_words = grouped[:].bitcast(F32)
@@ -243,7 +262,8 @@ def tile_decoder_pa_kernel(tc, h6_pre, g6, be6, W7, b7, out):
             width = STORE_WIDTHS[b]
             col = side * HALF + q * STEP
             if col % width == 0:
-                out_tiles[b] = out_pool.tile([P, 2 * width], F32, name="out_tile")
+                pool = fine_pool if width == STEP else out_pool
+                out_tiles[b] = pool.tile([P, 2 * width], F32, name="out_tile")
             tile = out_tiles[b]
             both = tile[:].rearrange("p (l j) -> p l j", l=2)
             rows = out[b].rearrange("(m l) j -> m l j", l=2)

@@ -24,7 +24,7 @@ HALF = 2 * STEP
 STEPS = BLOCKS * COLS // STEP
 HALVES = BLOCKS * COLS // HALF
 W_AHEAD = 8
-SPREAD_HALVES = 4
+SPREAD_HALVES = range(3, HALVES, 4)
 STORE_WIDTHS = [COLS] * (BLOCKS - 2) + [HALF, STEP]
 LAG = 2
 G_ROW, BE_ROW = STEPS, STEPS + BLOCKS
@@ -50,7 +50,7 @@ def tile_decoder_pa_kernel(tc, h6_pre, g6, be6, W7, b7, out):
         make_identity(nc, ident[:])
         ident_bf16 = keep.tile([P, P], BF16, name="ident_bf16")
         nc.gpsimd.tensor_copy(out=ident_bf16[:], in_=ident[:])
-        minus_half = keep.tile([P, PACK], F32, name="minus_half")
+        minus_half = keep.tile([P, PACK * 4], F32, name="minus_half")
         nc.gpsimd.memset(minus_half[:], -0.5)
 
         h_rows = keep.tile([P, BLOCKS * 2 * K], BF16, name="h_rows")
@@ -67,7 +67,7 @@ def tile_decoder_pa_kernel(tc, h6_pre, g6, be6, W7, b7, out):
         def load_w(half):
             b, side = divmod(half, 2)
             tile = w_pool.tile([P, HALF * K // P], BF16, name="w_rows")
-            if b < BLOCKS - 1:
+            if STORE_WIDTHS[b] > STEP:
                 nc.sync.dma_start(
                     out=tile[:].rearrange("p (i k) -> p i k", k=K),
                     in_=W7[b].rearrange("(d c i) k -> d c i k", d=2, c=P)[side],
@@ -140,14 +140,16 @@ def tile_decoder_pa_kernel(tc, h6_pre, g6, be6, W7, b7, out):
                     out=stats[:, (b * 2 + u) * 6 : (b * 2 + u + 1) * 6],
                     in_=h_flipped[b][:, u * 2 * ROWS : (u + 1) * 2 * ROWS],
                 )
-            four = slice(PACK * b, PACK * b + PACK)
-            g_four = slice(PACK * (G_ROW + b), PACK * (G_ROW + b + 1))
-            be_four = slice(PACK * (BE_ROW + b), PACK * (BE_ROW + b + 1))
+
+        def scale_and_shift(first, last):
+            four = slice(PACK * first, PACK * last)
+            g_four = slice(PACK * (G_ROW + first), PACK * (G_ROW + last))
+            be_four = slice(PACK * (BE_ROW + first), PACK * (BE_ROW + last))
             nc.gpsimd.tensor_scalar(
                 out=var_eps[:, four], in0=stats_view[:, four, 2], scalar1=1.0 / ROWS, scalar2=EPS,
                 op0=ALU.mult, op1=ALU.add,
             )
-            nc.gpsimd.tensor_tensor(out=inv_std[:, four], in0=var_eps[:, four], in1=minus_half[:], op=ALU.pow)
+            nc.gpsimd.tensor_tensor(out=inv_std[:, four], in0=var_eps[:, four], in1=minus_half[:, 0 : PACK * (last - first)], op=ALU.pow)
             nc.gpsimd.tensor_tensor(out=scale[:, four], in0=inv_std[:, four], in1=small_values[:, g_four], op=ALU.mult)
             nc.gpsimd.tensor_tensor(
                 out=mean_scaled[:, four], in0=stats_view[:, four, 1], in1=scale[:, four], op=ALU.mult
@@ -228,7 +230,7 @@ def tile_decoder_pa_kernel(tc, h6_pre, g6, be6, W7, b7, out):
         def transpose_w(step, copy):
             half, q = divmod(step, 2)
             if q == 0:
-                (spread_bias if half < SPREAD_HALVES else select_bias)(half)
+                (spread_bias if half in SPREAD_HALVES else select_bias)(half)
             words = w_rows[half][:].bitcast(F32)
             grouped = grouped_pool.tile([P, STEP * PACK], BF16, name="w_grouped", align_bytes=64)
             grouped_words = grouped[:].bitcast(F32)
@@ -296,9 +298,12 @@ def tile_decoder_pa_kernel(tc, h6_pre, g6, be6, W7, b7, out):
         transpose_h(0)
         transpose_small()
         statistics(0)
+        scale_and_shift(0, 1)
         for b in range(1, 4):
             transpose_h(b)
             statistics(b)
+            if b % 2 == 1:
+                scale_and_shift(max(1, b - 1), b + 1)
         transpose_w(0, nc.scalar.copy)
         quantise_w(0)
         normalise(0)
@@ -325,5 +330,7 @@ def tile_decoder_pa_kernel(tc, h6_pre, g6, be6, W7, b7, out):
                     quantise_a(b)
             if step < 6:
                 statistics(step + 2)
+            if step == 5:
+                scale_and_shift(4, 8)
         for step in range(STEPS - LAG, STEPS):
             multiply(step)

from contextlib import ExitStack

import concourse.mybir as mybir
from concourse.masks import make_identity

F32 = mybir.dt.float32
BF16 = mybir.dt.bfloat16
U32 = mybir.dt.uint32
U8 = mybir.dt.uint8
FP8X4 = mybir.dt.float8_e4m3fn_x4
ACT = mybir.ActivationFunctionType
ALU = mybir.AluOpType

P = 128
BLOCKS, ROWS, K, COLS = 8, 256, 512, 2048
EPS = 1e-5
FLOPS = 2 * BLOCKS * ROWS * K * COLS

PACK = 4
WORDS = K // 2
BANK = 512
STEP = 512
HALF = 2 * STEP
STEPS = BLOCKS * COLS // STEP
HALVES = BLOCKS * COLS // HALF
W_AHEAD = 8
SPREAD_HALVES = range(3, HALVES, 4)
STORE_WIDTHS = [COLS] * (BLOCKS - 2) + [HALF, STEP]
LAG = 2
G_ROW, BE_ROW = STEPS, STEPS + BLOCKS
SMALL = STEPS + 2 * BLOCKS


def tile_decoder_pa_kernel(tc, h6_pre, g6, be6, W7, b7, out):
    nc = tc.nc
    with ExitStack() as ctx:
        keep = ctx.enter_context(tc.tile_pool(name="keep", bufs=1))
        w_pool = ctx.enter_context(tc.tile_pool(name="w_rows", bufs=W_AHEAD))
        grouped_pool = ctx.enter_context(tc.tile_pool(name="w_grouped", bufs=6))
        code_pool = ctx.enter_context(tc.tile_pool(name="w_codes", bufs=6))
        a_pool = ctx.enter_context(tc.tile_pool(name="a_values", bufs=2))
        bias_pool = ctx.enter_context(tc.tile_pool(name="bias", bufs=3))
        out_pool = ctx.enter_context(tc.tile_pool(name="out_tiles", bufs=3))
        fine_pool = ctx.enter_context(tc.tile_pool(name="fine_out_tiles", bufs=4))
        flip_pool = ctx.enter_context(tc.psum_pool(name="flipped", bufs=4))
        acc_pool = ctx.enter_context(tc.psum_pool(name="sums", bufs=4))
        ctx.enter_context(tc.manual_schedule())

        ident = keep.tile([P, P], F32, name="ident")
        make_identity(nc, ident[:])
        ident_bf16 = keep.tile([P, P], BF16, name="ident_bf16")
        nc.gpsimd.tensor_copy(out=ident_bf16[:], in_=ident[:])
        minus_half = keep.tile([P, PACK * 4], F32, name="minus_half")
        nc.gpsimd.memset(minus_half[:], -0.5)

        h_rows = keep.tile([P, BLOCKS * 2 * K], BF16, name="h_rows")
        h_words = h_rows[:].bitcast(F32)

        def load_h(first, last):
            nc.sync.dma_start(
                out=h_rows[:, first * 2 * K : last * 2 * K].rearrange("p (b l k) -> p b l k", l=2, k=K),
                in_=h6_pre[first:last].rearrange("b (m l) k -> m b l k", l=2),
            )

        w_rows = {}

        def load_w(half):
            b, side = divmod(half, 2)
            tile = w_pool.tile([P, HALF * K // P], BF16, name="w_rows")
            if STORE_WIDTHS[b] > STEP:
                nc.sync.dma_start(
                    out=tile[:].rearrange("p (i k) -> p i k", k=K),
                    in_=W7[b].rearrange("(d c i) k -> d c i k", d=2, c=P)[side],
                )
            else:
                nc.sync.dma_start(
                    out=tile[:].rearrange("p (q a k) -> p q a k", q=2, a=4),
                    in_=W7[b].rearrange("(q c a) k -> c q a k", q=4, c=P)[:, 2 * side : 2 * side + 2],
                )
            w_rows[half] = tile

        small_rows = keep.tile([P, K], BF16, name="small_rows")
        nc.vector.memset(small_rows[32:64, :], 0.0)
        nc.vector.memset(small_rows[64:128, :], 0.0)
        load_h(0, 1)
        nc.sync.dma_start(out=small_rows[G_ROW : G_ROW + BLOCKS, :], in_=g6)
        nc.sync.dma_start(out=small_rows[BE_ROW : BE_ROW + BLOCKS, :], in_=be6)
        nc.sync.dma_start(out=small_rows[0:STEPS, :], in_=b7.rearrange("b (q w) -> (b q) w", w=STEP))
        load_h(1, 2)
        load_h(2, 4)
        load_w(0)
        load_h(4, 6)
        load_w(1)
        load_h(6, 8)
        for half in range(2, W_AHEAD):
            load_w(half)

        stats = keep.tile([P, BLOCKS * PACK * 3], F32, name="stats")
        stats_view = stats[:].rearrange("p (i c) -> p i c", c=3)
        var_eps = keep.tile([P, BLOCKS * PACK], F32, name="var_eps")
        inv_std = keep.tile([P, BLOCKS * PACK], F32, name="inv_std")
        scale = keep.tile([P, BLOCKS * PACK], F32, name="scale")
        mean_scaled = keep.tile([P, BLOCKS * PACK], F32, name="mean_scaled")
        shift = keep.tile([P, BLOCKS * PACK], F32, name="shift")
        small_cols = keep.tile([P, 2 * SMALL], F32, name="small_cols")
        small_values = small_cols[:].bitcast(BF16)
        h_flipped = {}
        a_planes = {}
        a_grouped = {}
        a_codes = {}

        def transpose_h(b):
            bank = flip_pool.tile([P, BANK], F32, name="bank", tag="bank")
            for u in range(2):
                for l in range(2):
                    first = (b * 2 + l) * WORDS
                    nc.tensor.transpose(
                        out=bank[:, (u * 2 + l) * P : (u * 2 + l + 1) * P],
                        in_=h_words[:, first + u : first + WORDS : 2],
                        identity=ident[:],
                    )
            flipped = keep.tile([P, BANK], F32, name="h_flipped%d" % b)
            nc.scalar.copy(out=flipped[:], in_=bank[:])
            h_flipped[b] = flipped[:].bitcast(BF16)

        def transpose_small():
            bank = flip_pool.tile([P, BANK], F32, name="bank", tag="bank")
            for u in range(2):
                nc.tensor.transpose(
                    out=bank[:, u * P : (u + 1) * P], in_=small_rows[:].bitcast(F32)[:, u:WORDS:2], identity=ident[:]
                )
            nc.scalar.copy(
                out=small_cols[:].rearrange("p (r u) -> p r u", u=2),
                in_=bank[:, 0 : 2 * P].rearrange("p (u r) -> p r u", u=2)[:, 0:SMALL, :],
            )

        def statistics(b):
            for u in range(2):
                nc.vector.bn_stats(
                    out=stats[:, (b * 2 + u) * 6 : (b * 2 + u + 1) * 6],
                    in_=h_flipped[b][:, u * 2 * ROWS : (u + 1) * 2 * ROWS],
                )

        def scale_and_shift(first, last):
            four = slice(PACK * first, PACK * last)
            g_four = slice(PACK * (G_ROW + first), PACK * (G_ROW + last))
            be_four = slice(PACK * (BE_ROW + first), PACK * (BE_ROW + last))
            nc.gpsimd.tensor_scalar(
                out=var_eps[:, four], in0=stats_view[:, four, 2], scalar1=1.0 / ROWS, scalar2=EPS,
                op0=ALU.mult, op1=ALU.add,
            )
            nc.gpsimd.tensor_tensor(out=inv_std[:, four], in0=var_eps[:, four], in1=minus_half[:, 0 : PACK * (last - first)], op=ALU.pow)
            nc.gpsimd.tensor_tensor(out=scale[:, four], in0=inv_std[:, four], in1=small_values[:, g_four], op=ALU.mult)
            nc.gpsimd.tensor_tensor(
                out=mean_scaled[:, four], in0=stats_view[:, four, 1], in1=scale[:, four], op=ALU.mult
            )
            nc.gpsimd.tensor_tensor(
                out=shift[:, four],
                in0=small_values[:, be_four],
                in1=mean_scaled[:, four],
                op=ALU.subtract,
            )

        def normalise(b):
            planes = a_pool.tile([P, PACK * ROWS], BF16, name="a_planes")
            for u in range(2):
                pairs = h_flipped[b][:, u * 2 * ROWS : (u + 1) * 2 * ROWS].rearrange("p (n e) -> p n e", e=2)
                for e in range(2):
                    t = 2 * u + e
                    nc.scalar.activation(
                        out=planes[:, t * ROWS : (t + 1) * ROWS],
                        in_=pairs[:, :, e],
                        func=ACT.Relu,
                        scale=scale[:, PACK * b + t : PACK * b + t + 1],
                        bias=shift[:, PACK * b + t : PACK * b + t + 1],
                    )
            a_planes[b] = planes

        def regroup(b):
            grouped = a_pool.tile([P, ROWS * PACK], BF16, name="a_grouped", align_bytes=64)
            copy = nc.scalar.copy if b % 2 == 1 else nc.vector.tensor_copy
            copy(
                out=grouped[:].rearrange("p (c i t) -> p c t i", i=4, t=PACK),
                in_=a_planes[b][:].rearrange("p (t c i) -> p c t i", t=PACK, i=4),
            )
            a_grouped[b] = grouped

        def quantise_a(b):
            codes = keep.tile([P, ROWS], U32, name="a_codes%d" % b, align_bytes=64)
            scales = keep.tile([P, ROWS], U8, name="a_scales%d" % b, align_bytes=64)
            nc.vector.quantize_mx(out=codes[:].bitcast(FP8X4), scales=scales[:], in_=a_grouped[b][:])
            a_codes[b] = (codes, scales)

        bias_tiles = {}
        w_grouped = {}
        w_codes = {}
        out_tiles = {}

        def spread_bias(half):
            bank = flip_pool.tile([P, BANK], F32, name="bank", tag="bank")
            for i in range(4):
                column = 4 * half + i
                nc.tensor.transpose(
                    out=bank[:, i * P : (i + 1) * P],
                    in_=small_cols[:, column : column + 1].to_broadcast([P, P]),
                    identity=ident[:],
                )
            spread = bias_pool.tile([P, BANK], F32, name="bias")
            nc.scalar.copy(
                out=spread[:].rearrange("p (q c u) -> p q c u", q=2, u=2),
                in_=bank[:].rearrange("p (q u c) -> p q c u", q=2, u=2),
            )
            bias_tiles[half] = spread[:].bitcast(BF16)

        def select_bias(half):
            bank = flip_pool.tile([P, HALF], BF16, name="bank", tag="bank")
            for q in range(2):
                row = 2 * half + q
                nc.tensor.matmul(
                    out=bank[:, q * STEP : (q + 1) * STEP],
                    lhsT=ident_bf16[:, row : row + 1].to_broadcast([P, P]),
                    rhs=small_rows[:],
                    start=True,
                    stop=True,
                )
            spread = bias_pool.tile([P, BANK], F32, name="bias")
            nc.scalar.copy(out=spread[:], in_=bank[:].bitcast(F32))
            bias_tiles[half] = spread[:].bitcast(BF16)

        def transpose_w(step, copy):
            half, q = divmod(step, 2)
            if q == 0:
                (spread_bias if half in SPREAD_HALVES else select_bias)(half)
            words = w_rows[half][:].bitcast(F32)
            grouped = grouped_pool.tile([P, STEP * PACK], BF16, name="w_grouped", align_bytes=64)
            grouped_words = grouped[:].bitcast(F32)
            for pair in range(2):
                bank = flip_pool.tile([P, BANK], F32, name="bank", tag="bank")
                for a in range(2):
                    for u in range(2):
                        first = (q * 4 + 2 * pair + a) * WORDS
                        nc.tensor.transpose(
                            out=bank[:, (a * 2 + u) * P : (a * 2 + u + 1) * P],
                            in_=words[:, first + u : first + WORDS : 2],
                            identity=ident[:],
                        )
                copy(
                    out=grouped_words[:, pair * BANK : (pair + 1) * BANK].rearrange("p (a c u) -> p a c u", a=2, u=2),
                    in_=bank[:].rearrange("p (a u c) -> p a c u", a=2, u=2),
                )
            w_grouped[step] = grouped

        def quantise_w(step):
            codes = code_pool.tile([P, STEP], U32, name="w_codes", align_bytes=64)
            scales = code_pool.tile([P, STEP], U8, name="w_scales", align_bytes=64)
            nc.vector.quantize_mx(out=codes[:].bitcast(FP8X4), scales=scales[:], in_=w_grouped[step][:])
            w_codes[step] = (codes, scales)

        def multiply(step):
            half, q = divmod(step, 2)
            b, side = divmod(half, 2)
            codes, scales = a_codes[b]
            moving, moving_scales = w_codes[step]
            width = STORE_WIDTHS[b]
            col = side * HALF + q * STEP
            if col % width == 0:
                pool = fine_pool if width == STEP else out_pool
                out_tiles[b] = pool.tile([P, 2 * width], F32, name="out_tile")
            tile = out_tiles[b]
            both = tile[:].rearrange("p (l j) -> p l j", l=2)
            rows = out[b].rearrange("(m l) j -> m l j", l=2)
            for l in range(2):
                acc = acc_pool.tile([P, BANK], F32, name="acc")
                nc.tensor.matmul_mx(
                    out=acc[:],
                    lhsT=codes[:, l * P : (l + 1) * P].bitcast(FP8X4),
                    lhsT_scale=scales[:, l * P : (l + 1) * P],
                    rhs=moving[:].bitcast(FP8X4),
                    rhs_scale=moving_scales[:],
                    start=True,
                    stop=True,
                )
                sums = acc[:].rearrange("p (a c) -> p c a", a=4)
                if width == STEP:
                    part = both[:, l].rearrange("p (c a) -> p c a", a=4)
                    bias = bias_tiles[half][:, q * STEP : (q + 1) * STEP].rearrange("p (c a) -> p c a", a=4)
                else:
                    first = side * HALF % width
                    part = both[:, l, first : first + HALF].rearrange("p (c q a) -> p q c a", q=2, a=4)[:, q]
                    bias = bias_tiles[half].rearrange("p (c q a) -> p q c a", q=2, a=4)[:, q]
                nc.vector.tensor_tensor(out=part, in0=sums, in1=bias, op=ALU.add)
                if step == STEPS - 1:
                    nc.sync.dma_start(out=rows[:, l, col : col + STEP], in_=both[:, l])
            end = col + STEP
            if end % width == 0 and step < STEPS - 1:
                nc.sync.dma_start(out=rows[:, :, end - width : end], in_=both)

        transpose_h(0)
        transpose_small()
        statistics(0)
        scale_and_shift(0, 1)
        for b in range(1, 4):
            transpose_h(b)
            statistics(b)
            if b % 2 == 1:
                scale_and_shift(max(1, b - 1), b + 1)
        transpose_w(0, nc.scalar.copy)
        quantise_w(0)
        normalise(0)
        transpose_w(1, nc.vector.tensor_copy)
        load_w(W_AHEAD)
        regroup(0)
        quantise_a(0)
        quantise_w(1)
        prepare_from = [max(2, 4 * b - 3) for b in range(BLOCKS)]
        for step in range(2, STEPS):
            transpose_w(step, nc.scalar.copy)
            quantise_w(step)
            if step < 6:
                transpose_h(step + 2)
            multiply(step - LAG)
            if step % 2 == 1 and step // 2 + W_AHEAD < HALVES:
                load_w(step // 2 + W_AHEAD)
            for b in range(1, BLOCKS):
                if step == prepare_from[b]:
                    normalise(b)
                if step == prepare_from[b] + 1:
                    regroup(b)
                if step == prepare_from[b] + 2:
                    quantise_a(b)
            if step < 6:
                statistics(step + 2)
            if step == 5:
                scale_and_shift(4, 8)
        for step in range(STEPS - LAG, STEPS):
            multiply(step)
